import numpy as np
import ml_dtypes


def mxq(x, axis, fmt="e4m3"):
    dtype, down = {"e4m3": (ml_dtypes.float8_e4m3fn, 7), "e5m2": (ml_dtypes.float8_e5m2, 14)}[fmt]
    v = np.moveaxis(np.asarray(x, np.float32).astype(ml_dtypes.bfloat16).astype(np.float64), axis, -1)
    blocks = v.reshape(v.shape[:-1] + (-1, 32))
    amax = np.abs(blocks).max(-1, keepdims=True)
    byte = np.maximum(np.where(amax > 0, np.frexp(amax)[1] - 1 + 127, 0) - down, 1)
    scale = np.exp2(byte - 127.0)
    codes = (blocks / scale).astype(np.float32).astype(dtype).astype(np.float64)
    return np.moveaxis((codes * scale).reshape(v.shape), -1, axis)


WIDE = False


def mx_kscale(k):
    if not WIDE:
        return np.ones(k)
    levels = np.array([10, -10, 5, -5, 0])
    a = np.random.permutation(np.resize(levels, k // 512 * 4)).reshape(k // 512, 4)
    idx = np.arange(k)
    return np.exp2(a[idx // 512, idx % 128 // 32])


BF16 = ml_dtypes.bfloat16


def bf(x):
    return np.asarray(x, np.float32).astype(BF16)


def f64(x):
    return np.asarray(x).astype(np.float64)


B, C, NH, GW, GH, GZ = 4, 512, 1, 16, 16, 8
N = GW * GH * GZ
D = C // NH
XS = 2.0


def setup_inputs():
    s, t = mx_kscale(C), mx_kscale(D)
    g = np.random.standard_normal((B, NH, D, D)) * np.sqrt(1.0 + C / N)
    e = np.exp(g - g.max(-1, keepdims=True))
    attn = e / e.sum(-1, keepdims=True)
    return {"x": bf(XS * np.random.standard_normal((B, C, GW, GH, GZ)) * s[None, :, None, None, None]),
            "w_v": bf(np.random.standard_normal((C, C)) / np.sqrt(C) / s[:, None] * np.tile(t, NH)[None, :]),
            "attn": bf(attn / t)}


def reference(x, w_v, attn):
    xt = f64(x).reshape(B, C, N).transpose(0, 2, 1)
    v = mxq(xt, 2, "e4m3") @ mxq(f64(w_v), 0, "e4m3")
    v = v.reshape(B, N, NH, D).transpose(0, 2, 3, 1)
    out = mxq(f64(attn), 3, "e4m3") @ mxq(v, 2, "e4m3")
    out = out.transpose(0, 3, 1, 2).reshape(B, N, C)
    return out.reshape(B, GW, GH, GZ, C).transpose(0, 4, 1, 2, 3)

@@ -1,0 +1,229 @@
+from contextlib import ExitStack
+
+import concourse.mybir as mybir
+from concourse.masks import make_identity
+
+BF16 = mybir.dt.bfloat16
+F32 = mybir.dt.float32
+U32 = mybir.dt.uint32
+U8 = mybir.dt.uint8
+FP8X4 = mybir.dt.float8_e4m3fn_x4
+
+P = 128
+PACK = 4
+SAMPLES = 4
+CHANNELS = P * PACK
+VOXELS = 16 * 16 * 8
+CHUNK = 512
+SLICE = CHUNK // PACK
+CHUNKS_PER_SAMPLE = VOXELS // CHUNK
+STEPS = SAMPLES * CHUNKS_PER_SAMPLE
+OUT_BUFFERS = 6
+
+FLOPS = 2 * 2 * SAMPLES * VOXELS * CHANNELS * CHANNELS
+
+
+def tile_channelattention_pb_t_kernel(tc, x, w_v, attn, out):
+    nc = tc.nc
+
+    x_rows = x.rearrange("b (p t) gw gh gz -> b p t (gw gh gz)", t=PACK)
+    w_rows = w_v.rearrange("(p t) j -> p t j", t=PACK)
+    out_rows = out.rearrange("b (p g) gw gh gz -> b p g (gw gh gz)", g=PACK)
+
+    with ExitStack() as ctx:
+        resident = ctx.enter_context(tc.tile_pool(name="resident", bufs=1))
+        stream = ctx.enter_context(tc.tile_pool(name="stream", bufs=3))
+        attn_pool = ctx.enter_context(tc.tile_pool(name="attn_pool", bufs=2))
+        out_pool = ctx.enter_context(tc.tile_pool(name="out_pool", bufs=OUT_BUFFERS))
+        psum_v = ctx.enter_context(tc.psum_pool(name="psum_v", bufs=4))
+        psum_o = ctx.enter_context(tc.psum_pool(name="psum_o", bufs=4))
+        ctx.enter_context(tc.manual_schedule())
+
+        w_raw = resident.tile([P, PACK, CHANNELS], BF16)
+        x_raw = [resident.tile([P, PACK, VOXELS], BF16, name="x_raw%d" % b) for b in range(SAMPLES)]
+        attn_raw = [
+            resident.tile([P, PACK * CHANNELS], BF16, name="attn_raw%d" % b) for b in range(SAMPLES)
+        ]
+
+        def load_x(b, first_chunk, chunks):
+            cols = slice(first_chunk * CHUNK, (first_chunk + chunks) * CHUNK)
+            nc.sync.dma_start(out=x_raw[b][:, :, cols], in_=x_rows[b, :, :, cols])
+
+        def load_attn(b):
+            nc.sync.dma_start(
+                out=attn_raw[b][:], in_=attn[b, 0].rearrange("(p g) j -> p (g j)", g=PACK)
+            )
+
+        nc.sync.dma_start(out=w_raw[:], in_=w_rows)
+        load_x(0, 0, 1)
+        load_attn(0)
+        for chunk in range(1, CHUNKS_PER_SAMPLE):
+            load_x(0, chunk, 1)
+        for b in range(1, SAMPLES):
+            load_x(b, 0, CHUNKS_PER_SAMPLE)
+            load_attn(b)
+
+        identity = resident.tile([P, P], F32)
+        make_identity(nc, identity[:])
+
+        w_grouped = resident.tile([P, PACK, P, PACK], BF16, align_bytes=64)
+        w_codes = resident.tile([P, CHANNELS], U32, align_bytes=64)
+        w_scales = resident.tile([P, CHANNELS], U8, align_bytes=64)
+
+        def regroup_w():
+            nc.scalar.copy(
+                out=w_grouped[:].rearrange("p s m t -> p m t s"),
+                in_=w_raw[:].rearrange("p t (m s) -> p m t s", s=PACK),
+            )
+
+        def quantise_w():
+            nc.vector.quantize_mx(
+                out=w_codes[:].bitcast(FP8X4),
+                scales=w_scales[:],
+                in_=w_grouped[:].rearrange("p s m t -> p (s m t)"),
+            )
+
+        attn_grouped = {}
+        attn_mx = {}
+
+        def transpose_attn(b):
+            words = attn_raw[b][:].bitcast(F32).rearrange("p (g m u) -> p g u m", g=PACK, u=2)
+            grouped = attn_pool.tile([P, PACK * P * PACK], BF16, align_bytes=64, name="attn_grouped")
+            grouped_words = grouped[:].bitcast(F32).rearrange("m (g p u) -> m g p u", g=PACK, u=2)
+            for half in range(2):
+                bank = psum_o.tile([P, 2, 2, P], F32, tag="bank", name="attn_bank")
+                for g in range(2):
+                    for u in range(2):
+                        nc.tensor.transpose(bank[:, g, u, :], words[:, 2 * half + g, u, :], identity[:])
+                nc.scalar.copy(
+                    out=grouped_words[:, 2 * half : 2 * half + 2, :, :],
+                    in_=bank[:].rearrange("m g u p -> m g p u"),
+                )
+            attn_grouped[b] = grouped
+
+        def quantise_attn(b):
+            codes = attn_pool.tile([P, CHANNELS], U32, align_bytes=64, name="attn_codes")
+            scales = attn_pool.tile([P, CHANNELS], U8, align_bytes=64, name="attn_scales")
+            nc.vector.quantize_mx(out=codes[:].bitcast(FP8X4), scales=scales[:], in_=attn_grouped[b][:])
+            attn_mx[b] = (codes, scales)
+
+        x_grouped = {}
+        x_mx = {}
+        v_banks = {}
+        v_mx = {}
+        out_banks = {}
+
+        def regroup_x(k):
+            b, q = divmod(k, CHUNKS_PER_SAMPLE)
+            grouped = stream.tile([P, CHUNK, PACK], BF16, align_bytes=64, name="x_grouped")
+            nc.vector.tensor_copy(
+                out=grouped[:].rearrange("p (c i) t -> p c t i", i=4),
+                in_=x_raw[b][:, :, q * CHUNK : (q + 1) * CHUNK].rearrange("p t (c i) -> p c t i", i=4),
+            )
+            x_grouped[k] = grouped
+
+        def quantise_x(k):
+            codes = stream.tile([P, CHUNK], U32, align_bytes=64, name="x_codes")
+            scales = stream.tile([P, CHUNK], U8, align_bytes=64, name="x_scales")
+            nc.vector.quantize_mx(
+                out=codes[:].bitcast(FP8X4),
+                scales=scales[:],
+                in_=x_grouped[k][:].rearrange("p n t -> p (n t)"),
+            )
+            x_mx[k] = (codes, scales)
+
+        def first_product(k):
+            codes, scales = x_mx[k]
+            v_banks[k] = []
+            for r in range(PACK):
+                voxels = slice(r * SLICE, (r + 1) * SLICE)
+                bank = psum_v.tile([P, PACK, SLICE], F32, name="v_bank")
+                for s in range(PACK):
+                    tile_s = slice(s * P, (s + 1) * P)
+                    nc.tensor.matmul_mx(
+                        out=bank[:, s, :],
+                        lhsT=w_codes[:, tile_s].bitcast(FP8X4),
+                        lhsT_scale=w_scales[:, tile_s],
+                        rhs=codes[:, voxels].bitcast(FP8X4),
+                        rhs_scale=scales[:, voxels],
+                        start=True,
+                        stop=True,
+                    )
+                v_banks[k].append(bank)
+
+        v_grouped = {}
+
+        def round_v(k):
+            grouped = stream.tile([P, CHUNK, PACK], BF16, align_bytes=64, name="v_grouped")
+            for r in range(PACK):
+                dst = grouped[:, r * SLICE : (r + 1) * SLICE, :]
+                src = v_banks[k][r][:].rearrange("m s n -> m n s")
+                if r < PACK // 2:
+                    nc.scalar.copy(out=dst, in_=src)
+                else:
+                    nc.vector.tensor_copy(out=dst, in_=src)
+            v_grouped[k] = grouped
+
+        def quantise_v(k):
+            codes = stream.tile([P, CHUNK], U32, align_bytes=64, name="v_codes")
+            scales = stream.tile([P, CHUNK], U8, align_bytes=64, name="v_scales")
+            nc.vector.quantize_mx(
+                out=codes[:].bitcast(FP8X4),
+                scales=scales[:],
+                in_=v_grouped[k][:].rearrange("m n s -> m (n s)"),
+            )
+            v_mx[k] = (codes, scales)
+
+        def second_product(k):
+            a_codes, a_scales = attn_mx[k // CHUNKS_PER_SAMPLE]
+            codes, scales = v_mx[k]
+            out_banks[k] = []
+            for g in range(PACK):
+                tile_g = slice(g * P, (g + 1) * P)
+                bank = psum_o.tile([P, CHUNK], F32, tag="bank", name="out_bank")
+                nc.tensor.matmul_mx(
+                    out=bank[:],
+                    lhsT=a_codes[:, tile_g].bitcast(FP8X4),
+                    lhsT_scale=a_scales[:, tile_g],
+                    rhs=codes[:].bitcast(FP8X4),
+                    rhs_scale=scales[:],
+                    start=True,
+                    stop=True,
+                )
+                out_banks[k].append(bank)
+
+        def store_out(k):
+            b, q = divmod(k, CHUNKS_PER_SAMPLE)
+            result = out_pool.tile([P, PACK, CHUNK], F32, name="result")
+            for g in range(PACK):
+                if k == STEPS - 1 and g % 2 == 1:
+                    nc.vector.tensor_copy(out=result[:, g, :], in_=out_banks[k][g][:])
+                else:
+                    nc.scalar.copy(out=result[:, g, :], in_=out_banks[k][g][:])
+            nc.sync.dma_start(out=out_rows[b, :, :, q * CHUNK : (q + 1) * CHUNK], in_=result[:])
+
+        regroup_w()
+        regroup_x(0)
+        transpose_attn(0)
+        quantise_w()
+        quantise_x(0)
+        first_product(0)
+        for k in range(STEPS):
+            b, q = divmod(k, CHUNKS_PER_SAMPLE)
+            if k + 1 < STEPS:
+                regroup_x(k + 1)
+            round_v(k)
+            if k >= 1:
+                store_out(k - 1)
+            if q == 1 and b + 1 < SAMPLES:
+                transpose_attn(b + 1)
+            if k + 1 < STEPS:
+                quantise_x(k + 1)
+                first_product(k + 1)
+            if k == 0:
+                quantise_attn(0)
+            if q == 2 and b + 1 < SAMPLES:
+                quantise_attn(b + 1)
+            quantise_v(k)
+            second_product(k)
+        store_out(STEPS - 1)

@@ -18,7 +18,7 @@ CHUNK = 512
 SLICE = CHUNK // PACK
 CHUNKS_PER_SAMPLE = VOXELS // CHUNK
 STEPS = SAMPLES * CHUNKS_PER_SAMPLE
-OUT_BUFFERS = 6
+OUT_BUFFERS = 24
 
 FLOPS = 2 * 2 * SAMPLES * VOXELS * CHANNELS * CHANNELS
 
@@ -40,27 +40,28 @@ def tile_channelattention_pb_t_kernel(tc, x, w_v, attn, out):
         ctx.enter_context(tc.manual_schedule())
 
         w_raw = resident.tile([P, PACK, CHANNELS], BF16)
-        x_raw = [resident.tile([P, PACK, VOXELS], BF16, name="x_raw%d" % b) for b in range(SAMPLES)]
         attn_raw = [
             resident.tile([P, PACK * CHANNELS], BF16, name="attn_raw%d" % b) for b in range(SAMPLES)
         ]
-
-        def load_x(b, first_chunk, chunks):
-            cols = slice(first_chunk * CHUNK, (first_chunk + chunks) * CHUNK)
-            nc.sync.dma_start(out=x_raw[b][:, :, cols], in_=x_rows[b, :, :, cols])
 
         def load_attn(b):
             nc.sync.dma_start(
                 out=attn_raw[b][:], in_=attn[b, 0].rearrange("(p g) j -> p (g j)", g=PACK)
             )
 
+        x_chunk = []
         nc.sync.dma_start(out=w_raw[:], in_=w_rows)
-        load_x(0, 0, 1)
-        load_attn(0)
-        for chunk in range(1, CHUNKS_PER_SAMPLE):
-            load_x(0, chunk, 1)
+        for q in range(CHUNKS_PER_SAMPLE):
+            piece = resident.tile([P, PACK, CHUNK], BF16, name="x_piece%d" % q)
+            nc.sync.dma_start(out=piece[:], in_=x_rows[0, :, :, q * CHUNK : (q + 1) * CHUNK])
+            x_chunk.append(piece[:])
+            if q == 0:
+                load_attn(0)
         for b in range(1, SAMPLES):
-            load_x(b, 0, CHUNKS_PER_SAMPLE)
+            whole = resident.tile([P, PACK, VOXELS], BF16, name="x_whole%d" % b)
+            nc.sync.dma_start(out=whole[:], in_=x_rows[b])
+            for q in range(CHUNKS_PER_SAMPLE):
+                x_chunk.append(whole[:, :, q * CHUNK : (q + 1) * CHUNK])
             load_attn(b)
 
         identity = resident.tile([P, P], F32)
@@ -114,11 +115,10 @@ def tile_channelattention_pb_t_kernel(tc, x, w_v, attn, out):
         out_banks = {}
 
         def regroup_x(k):
-            b, q = divmod(k, CHUNKS_PER_SAMPLE)
             grouped = stream.tile([P, CHUNK, PACK], BF16, align_bytes=64, name="x_grouped")
             nc.vector.tensor_copy(
                 out=grouped[:].rearrange("p (c i) t -> p c t i", i=4),
-                in_=x_raw[b][:, :, q * CHUNK : (q + 1) * CHUNK].rearrange("p t (c i) -> p c t i", i=4),
+                in_=x_chunk[k].rearrange("p t (c i) -> p c t i", i=4),
             )
             x_grouped[k] = grouped
 
@@ -194,13 +194,13 @@ def tile_channelattention_pb_t_kernel(tc, x, w_v, attn, out):
 
         def store_out(k):
             b, q = divmod(k, CHUNKS_PER_SAMPLE)
-            result = out_pool.tile([P, PACK, CHUNK], F32, name="result")
             for g in range(PACK):
+                result = out_pool.tile([P, CHUNK], F32, name="result")
                 if k == STEPS - 1 and g % 2 == 1:
-                    nc.vector.tensor_copy(out=result[:, g, :], in_=out_banks[k][g][:])
+                    nc.vector.tensor_copy(out=result[:], in_=out_banks[k][g][:])
                 else:
-                    nc.scalar.copy(out=result[:, g, :], in_=out_banks[k][g][:])
-            nc.sync.dma_start(out=out_rows[b, :, :, q * CHUNK : (q + 1) * CHUNK], in_=result[:])
+                    nc.scalar.copy(out=result[:], in_=out_banks[k][g][:])
+                nc.sync.dma_start(out=out_rows[b, :, g, q * CHUNK : (q + 1) * CHUNK], in_=result[:])
 
         regroup_w()
         regroup_x(0)

@@ -158,7 +158,7 @@ def tile_channelattention_pb_t_kernel(tc, x, w_v, attn, out):
             for r in range(PACK):
                 dst = grouped[:, r * SLICE : (r + 1) * SLICE, :]
                 src = v_banks[k][r][:].rearrange("m s n -> m n s")
-                if r < PACK // 2:
+                if r < PACK // 2 or k == 0:
                     nc.scalar.copy(out=dst, in_=src)
                 else:
                     nc.vector.tensor_copy(out=dst, in_=src)
@@ -208,22 +208,25 @@ def tile_channelattention_pb_t_kernel(tc, x, w_v, attn, out):
         quantise_w()
         quantise_x(0)
         first_product(0)
+        regroup_x(1)
+        quantise_x(1)
         for k in range(STEPS):
             b, q = divmod(k, CHUNKS_PER_SAMPLE)
-            if k + 1 < STEPS:
-                regroup_x(k + 1)
             round_v(k)
+            if k + 1 < STEPS:
+                first_product(k + 1)
             if k >= 1:
                 store_out(k - 1)
             if q == 1 and b + 1 < SAMPLES:
                 transpose_attn(b + 1)
-            if k + 1 < STEPS:
-                quantise_x(k + 1)
-                first_product(k + 1)
+            if k + 2 < STEPS:
+                regroup_x(k + 2)
             if k == 0:
                 quantise_attn(0)
             if q == 2 and b + 1 < SAMPLES:
                 quantise_attn(b + 1)
             quantise_v(k)
             second_product(k)
+            if k + 2 < STEPS:
+                quantise_x(k + 2)
         store_out(STEPS - 1)

@@ -18,6 +18,8 @@ CHUNK = 512
 SLICE = CHUNK // PACK
 CHUNKS_PER_SAMPLE = VOXELS // CHUNK
 STEPS = SAMPLES * CHUNKS_PER_SAMPLE
+GPSIMD_VOXELS = 128
+GPSIMD_FIRST_CHUNK = 3
 OUT_BUFFERS = 24
 
 FLOPS = 2 * 2 * SAMPLES * VOXELS * CHANNELS * CHANNELS
@@ -116,9 +118,20 @@ def tile_channelattention_pb_t_kernel(tc, x, w_v, attn, out):
 
         def regroup_x(k):
             grouped = stream.tile([P, CHUNK, PACK], BF16, align_bytes=64, name="x_grouped")
+            split = CHUNK
+            if k >= GPSIMD_FIRST_CHUNK:
+                split = CHUNK - GPSIMD_VOXELS
+                nc.gpsimd.tensor_scalar(
+                    out=grouped[:, split:, :],
+                    in0=x_chunk[k][:, :, split:].rearrange("p t n -> p n t"),
+                    scalar1=1.0,
+                    scalar2=0.0,
+                    op0=mybir.AluOpType.mult,
+                    op1=mybir.AluOpType.add,
+                )
             nc.vector.tensor_copy(
-                out=grouped[:].rearrange("p (c i) t -> p c t i", i=4),
-                in_=x_chunk[k].rearrange("p t (c i) -> p c t i", i=4),
+                out=grouped[:, :split, :].rearrange("p (c i) t -> p c t i", i=4),
+                in_=x_chunk[k][:, :, :split].rearrange("p t (c i) -> p c t i", i=4),
             )
             x_grouped[k] = grouped
 
@@ -155,10 +168,15 @@ def tile_channelattention_pb_t_kernel(tc, x, w_v, attn, out):
 
         def round_v(k):
             grouped = stream.tile([P, CHUNK, PACK], BF16, align_bytes=64, name="v_grouped")
+            scalar_banks = 2
+            if k == 0:
+                scalar_banks = 4
+            if k % CHUNKS_PER_SAMPLE == 3:
+                scalar_banks = 1
             for r in range(PACK):
                 dst = grouped[:, r * SLICE : (r + 1) * SLICE, :]
                 src = v_banks[k][r][:].rearrange("m s n -> m n s")
-                if r < PACK // 2 or k == 0:
+                if r < scalar_banks:
                     nc.scalar.copy(out=dst, in_=src)
                 else:
                     nc.vector.tensor_copy(out=dst, in_=src)

@@ -16,6 +16,7 @@ CHANNELS = P * PACK
 VOXELS = 16 * 16 * 8
 CHUNK = 512
 SLICE = CHUNK // PACK
+HALF = CHUNK // 2
 CHUNKS_PER_SAMPLE = VOXELS // CHUNK
 STEPS = SAMPLES * CHUNKS_PER_SAMPLE
 GPSIMD_VOXELS = 128
@@ -51,19 +52,26 @@ def tile_channelattention_pb_t_kernel(tc, x, w_v, attn, out):
                 out=attn_raw[b][:], in_=attn[b, 0].rearrange("(p g) j -> p (g j)", g=PACK)
             )
 
-        x_chunk = []
+        x_part = []
+
+        def load_x(b, first, voxels):
+            piece = resident.tile([P, PACK, voxels], BF16, name="x_piece%d_%d" % (b, first))
+            nc.sync.dma_start(out=piece[:], in_=x_rows[b, :, :, first : first + voxels])
+            return piece
+
         nc.sync.dma_start(out=w_raw[:], in_=w_rows)
-        for q in range(CHUNKS_PER_SAMPLE):
-            piece = resident.tile([P, PACK, CHUNK], BF16, name="x_piece%d" % q)
-            nc.sync.dma_start(out=piece[:], in_=x_rows[0, :, :, q * CHUNK : (q + 1) * CHUNK])
-            x_chunk.append(piece[:])
-            if q == 0:
-                load_attn(0)
+        x_part.append([(h * HALF, HALF, load_x(0, h * HALF, HALF)[:]) for h in range(2)])
+        x_part.append([(0, CHUNK, load_x(0, CHUNK, CHUNK)[:])])
+        load_attn(0)
+        for q in range(2, CHUNKS_PER_SAMPLE):
+            x_part.append([(0, CHUNK, load_x(0, q * CHUNK, CHUNK)[:])])
         for b in range(1, SAMPLES):
-            whole = resident.tile([P, PACK, VOXELS], BF16, name="x_whole%d" % b)
-            nc.sync.dma_start(out=whole[:], in_=x_rows[b])
-            for q in range(CHUNKS_PER_SAMPLE):
-                x_chunk.append(whole[:, :, q * CHUNK : (q + 1) * CHUNK])
+            pieces = 2 if b == 1 else 1
+            span = VOXELS // pieces
+            for h in range(pieces):
+                piece = load_x(b, h * span, span)
+                for q in range(span // CHUNK):
+                    x_part.append([(0, CHUNK, piece[:, :, q * CHUNK : (q + 1) * CHUNK])])
             load_attn(b)
 
         identity = resident.tile([P, P], F32)
@@ -74,10 +82,10 @@ def tile_channelattention_pb_t_kernel(tc, x, w_v, attn, out):
         w_scales = resident.tile([P, CHANNELS], U8, align_bytes=64)
 
         def regroup_w():
-            nc.scalar.copy(
-                out=w_grouped[:].rearrange("p s m t -> p m t s"),
-                in_=w_raw[:].rearrange("p t (m s) -> p m t s", s=PACK),
-            )
+            dst = w_grouped[:].rearrange("p s m t -> p m t s")
+            src = w_raw[:].rearrange("p t (m s) -> p m t s", s=PACK)
+            nc.scalar.copy(out=dst[:, : P // 2], in_=src[:, : P // 2])
+            nc.vector.tensor_copy(out=dst[:, P // 2 :], in_=src[:, P // 2 :])
 
         def quantise_w():
             nc.vector.quantize_mx(
@@ -116,34 +124,39 @@ def tile_channelattention_pb_t_kernel(tc, x, w_v, attn, out):
         v_mx = {}
         out_banks = {}
 
-        def regroup_x(k):
-            grouped = stream.tile([P, CHUNK, PACK], BF16, align_bytes=64, name="x_grouped")
-            split = CHUNK
-            if k >= GPSIMD_FIRST_CHUNK:
-                split = CHUNK - GPSIMD_VOXELS
-                nc.gpsimd.tensor_scalar(
-                    out=grouped[:, split:, :],
-                    in0=x_chunk[k][:, :, split:].rearrange("p t n -> p n t"),
-                    scalar1=1.0,
-                    scalar2=0.0,
-                    op0=mybir.AluOpType.mult,
-                    op1=mybir.AluOpType.add,
+        def regroup_x(k, pieces=None):
+            if k not in x_grouped:
+                x_grouped[k] = stream.tile([P, CHUNK, PACK], BF16, align_bytes=64, name="x_grouped")
+            grouped = x_grouped[k]
+            for first, voxels, view in x_part[k] if pieces is None else [x_part[k][i] for i in pieces]:
+                split = voxels
+                if k >= GPSIMD_FIRST_CHUNK:
+                    split = voxels - GPSIMD_VOXELS
+                    nc.gpsimd.tensor_scalar(
+                        out=grouped[:, first + split : first + voxels, :],
+                        in0=view[:, :, split:].rearrange("p t n -> p n t"),
+                        scalar1=1.0,
+                        scalar2=0.0,
+                        op0=mybir.AluOpType.mult,
+                        op1=mybir.AluOpType.add,
+                    )
+                nc.vector.tensor_copy(
+                    out=grouped[:, first : first + split, :].rearrange("p (c i) t -> p c t i", i=4),
+                    in_=view[:, :, :split].rearrange("p t (c i) -> p c t i", i=4),
                 )
-            nc.vector.tensor_copy(
-                out=grouped[:, :split, :].rearrange("p (c i) t -> p c t i", i=4),
-                in_=x_chunk[k][:, :, :split].rearrange("p t (c i) -> p c t i", i=4),
-            )
-            x_grouped[k] = grouped
 
-        def quantise_x(k):
-            codes = stream.tile([P, CHUNK], U32, align_bytes=64, name="x_codes")
-            scales = stream.tile([P, CHUNK], U8, align_bytes=64, name="x_scales")
-            nc.vector.quantize_mx(
-                out=codes[:].bitcast(FP8X4),
-                scales=scales[:],
-                in_=x_grouped[k][:].rearrange("p n t -> p (n t)"),
-            )
-            x_mx[k] = (codes, scales)
+        def quantise_x(k, pieces=None):
+            if k not in x_mx:
+                x_codes = stream.tile([P, CHUNK], U32, align_bytes=64, name="x_codes")
+                x_scales = stream.tile([P, CHUNK], U8, align_bytes=64, name="x_scales")
+                x_mx[k] = (x_codes, x_scales)
+            codes, scales = x_mx[k]
+            for first, voxels, view in x_part[k] if pieces is None else [x_part[k][i] for i in pieces]:
+                nc.vector.quantize_mx(
+                    out=codes[:, first : first + voxels].bitcast(FP8X4),
+                    scales=scales[:, first : first + voxels],
+                    in_=x_grouped[k][:, first : first + voxels, :].rearrange("p n t -> p (n t)"),
+                )
 
         def first_product(k):
             codes, scales = x_mx[k]
@@ -171,6 +184,8 @@ def tile_channelattention_pb_t_kernel(tc, x, w_v, attn, out):
             scalar_banks = 2
             if k == 0:
                 scalar_banks = 4
+            if k == 1:
+                scalar_banks = 3
             if k % CHUNKS_PER_SAMPLE == 3:
                 scalar_banks = 1
             for r in range(PACK):
@@ -221,29 +236,35 @@ def tile_channelattention_pb_t_kernel(tc, x, w_v, attn, out):
                 nc.sync.dma_start(out=out_rows[b, :, g, q * CHUNK : (q + 1) * CHUNK], in_=result[:])
 
         regroup_w()
-        regroup_x(0)
-        transpose_attn(0)
+        regroup_x(0, [0])
         quantise_w()
-        quantise_x(0)
+        quantise_x(0, [0])
+        regroup_x(0, [1])
+        quantise_x(0, [1])
         first_product(0)
         regroup_x(1)
         quantise_x(1)
         for k in range(STEPS):
             b, q = divmod(k, CHUNKS_PER_SAMPLE)
             round_v(k)
+            if k == 0:
+                transpose_attn(0)
             if k + 1 < STEPS:
                 first_product(k + 1)
             if k >= 1:
                 store_out(k - 1)
-            if q == 1 and b + 1 < SAMPLES:
+            if q == 2 and b + 1 < SAMPLES:
                 transpose_attn(b + 1)
+            if k == 0:
+                quantise_v(k)
             if k + 2 < STEPS:
                 regroup_x(k + 2)
             if k == 0:
                 quantise_attn(0)
-            if q == 2 and b + 1 < SAMPLES:
+            if q == 3 and b + 1 < SAMPLES:
                 quantise_attn(b + 1)
-            quantise_v(k)
+            if k > 0:
+                quantise_v(k)
             second_product(k)
             if k + 2 < STEPS:
                 quantise_x(k + 2)

@@ -17,6 +17,7 @@ VOXELS = 16 * 16 * 8
 CHUNK = 512
 SLICE = CHUNK // PACK
 HALF = CHUNK // 2
+WARM_MATMULS = 10
 CHUNKS_PER_SAMPLE = VOXELS // CHUNK
 STEPS = SAMPLES * CHUNKS_PER_SAMPLE
 GPSIMD_VOXELS = 128
@@ -76,6 +77,12 @@ def tile_channelattention_pb_t_kernel(tc, x, w_v, attn, out):
 
         identity = resident.tile([P, P], F32)
         make_identity(nc, identity[:])
+
+        zeros = resident.tile([P, CHUNK], BF16)
+        nc.gpsimd.memset(zeros[:], 0.0)
+        warm_bank = psum_v.tile([P, CHUNK], F32, name="v_bank")
+        for i in range(WARM_MATMULS):
+            nc.tensor.matmul(warm_bank[:], lhsT=zeros[:, :P], rhs=zeros[:], start=True, stop=True)
 
         w_grouped = resident.tile([P, PACK, P, PACK], BF16, align_bytes=64)
         w_codes = resident.tile([P, CHANNELS], U32, align_bytes=64)
@@ -140,7 +147,8 @@ def tile_channelattention_pb_t_kernel(tc, x, w_v, attn, out):
                         op0=mybir.AluOpType.mult,
                         op1=mybir.AluOpType.add,
                     )
-                nc.vector.tensor_copy(
+                copy = nc.scalar.copy if (k == 0 and first > 0) else nc.vector.tensor_copy
+                copy(
                     out=grouped[:, first : first + split, :].rearrange("p (c i) t -> p c t i", i=4),
                     in_=view[:, :, :split].rearrange("p t (c i) -> p c t i", i=4),
                 )

@@ -20,7 +20,7 @@ HALF = CHUNK // 2
 WARM_MATMULS = 10
 CHUNKS_PER_SAMPLE = VOXELS // CHUNK
 STEPS = SAMPLES * CHUNKS_PER_SAMPLE
-GPSIMD_VOXELS = 128
+GPSIMD_VOXELS = 192
 GPSIMD_FIRST_CHUNK = 3
 OUT_BUFFERS = 24
 

@@ -21,7 +21,7 @@ WARM_MATMULS = 10
 CHUNKS_PER_SAMPLE = VOXELS // CHUNK
 STEPS = SAMPLES * CHUNKS_PER_SAMPLE
 GPSIMD_VOXELS = 192
-GPSIMD_FIRST_CHUNK = 3
+GPSIMD_FIRST_CHUNK = 4
 OUT_BUFFERS = 24
 
 FLOPS = 2 * 2 * SAMPLES * VOXELS * CHANNELS * CHANNELS
@@ -37,6 +37,7 @@ def tile_channelattention_pb_t_kernel(tc, x, w_v, attn, out):
     with ExitStack() as ctx:
         resident = ctx.enter_context(tc.tile_pool(name="resident", bufs=1))
         stream = ctx.enter_context(tc.tile_pool(name="stream", bufs=3))
+        grouped_pool = ctx.enter_context(tc.tile_pool(name="grouped_pool", bufs=3))
         attn_pool = ctx.enter_context(tc.tile_pool(name="attn_pool", bufs=2))
         out_pool = ctx.enter_context(tc.tile_pool(name="out_pool", bufs=OUT_BUFFERS))
         psum_v = ctx.enter_context(tc.psum_pool(name="psum_v", bufs=4))
@@ -133,7 +134,7 @@ def tile_channelattention_pb_t_kernel(tc, x, w_v, attn, out):
 
         def regroup_x(k, pieces=None):
             if k not in x_grouped:
-                x_grouped[k] = stream.tile([P, CHUNK, PACK], BF16, align_bytes=64, name="x_grouped")
+                x_grouped[k] = grouped_pool.tile([P, CHUNK, PACK], BF16, align_bytes=64, name="grouped")
             grouped = x_grouped[k]
             for first, voxels, view in x_part[k] if pieces is None else [x_part[k][i] for i in pieces]:
                 split = voxels
@@ -188,7 +189,7 @@ def tile_channelattention_pb_t_kernel(tc, x, w_v, attn, out):
         v_grouped = {}
 
         def round_v(k):
-            grouped = stream.tile([P, CHUNK, PACK], BF16, align_bytes=64, name="v_grouped")
+            grouped = grouped_pool.tile([P, CHUNK, PACK], BF16, align_bytes=64, name="grouped")
             scalar_banks = 2
             if k == 0:
                 scalar_banks = 4

@@ -132,6 +132,16 @@ def tile_channelattention_pb_t_kernel(tc, x, w_v, attn, out):
         v_mx = {}
         out_banks = {}
 
+        def vector_banks(k):
+            if k < 2:
+                return k
+            if k % CHUNKS_PER_SAMPLE == 3 or k == 13:
+                return 3
+            return 2
+
+        def gpsimd_voxels(k):
+            return GPSIMD_VOXELS * vector_banks(k - 2) // 2
+
         def regroup_x(k, pieces=None):
             if k not in x_grouped:
                 x_grouped[k] = grouped_pool.tile([P, CHUNK, PACK], BF16, align_bytes=64, name="grouped")
@@ -139,7 +149,7 @@ def tile_channelattention_pb_t_kernel(tc, x, w_v, attn, out):
             for first, voxels, view in x_part[k] if pieces is None else [x_part[k][i] for i in pieces]:
                 split = voxels
                 if k >= GPSIMD_FIRST_CHUNK:
-                    split = voxels - GPSIMD_VOXELS
+                    split = voxels - gpsimd_voxels(k)
                     nc.gpsimd.tensor_scalar(
                         out=grouped[:, first + split : first + voxels, :],
                         in0=view[:, :, split:].rearrange("p t n -> p n t"),
@@ -190,13 +200,7 @@ def tile_channelattention_pb_t_kernel(tc, x, w_v, attn, out):
 
         def round_v(k):
             grouped = grouped_pool.tile([P, CHUNK, PACK], BF16, align_bytes=64, name="grouped")
-            scalar_banks = 2
-            if k == 0:
-                scalar_banks = 4
-            if k == 1:
-                scalar_banks = 3
-            if k % CHUNKS_PER_SAMPLE == 3:
-                scalar_banks = 1
+            scalar_banks = PACK - vector_banks(k)
             for r in range(PACK):
                 dst = grouped[:, r * SLICE : (r + 1) * SLICE, :]
                 src = v_banks[k][r][:].rearrange("m s n -> m n s")

from contextlib import ExitStack

import concourse.mybir as mybir
from concourse.masks import make_identity

BF16 = mybir.dt.bfloat16
F32 = mybir.dt.float32
U32 = mybir.dt.uint32
U8 = mybir.dt.uint8
FP8X4 = mybir.dt.float8_e4m3fn_x4

P = 128
PACK = 4
SAMPLES = 4
CHANNELS = P * PACK
VOXELS = 16 * 16 * 8
CHUNK = 512
SLICE = CHUNK // PACK
HALF = CHUNK // 2
WARM_MATMULS = 10
CHUNKS_PER_SAMPLE = VOXELS // CHUNK
STEPS = SAMPLES * CHUNKS_PER_SAMPLE
GPSIMD_VOXELS = 192
GPSIMD_FIRST_CHUNK = 4
OUT_BUFFERS = 24

FLOPS = 2 * 2 * SAMPLES * VOXELS * CHANNELS * CHANNELS


def tile_channelattention_pb_t_kernel(tc, x, w_v, attn, out):
    nc = tc.nc

    x_rows = x.rearrange("b (p t) gw gh gz -> b p t (gw gh gz)", t=PACK)
    w_rows = w_v.rearrange("(p t) j -> p t j", t=PACK)
    out_rows = out.rearrange("b (p g) gw gh gz -> b p g (gw gh gz)", g=PACK)

    with ExitStack() as ctx:
        resident = ctx.enter_context(tc.tile_pool(name="resident", bufs=1))
        stream = ctx.enter_context(tc.tile_pool(name="stream", bufs=3))
        grouped_pool = ctx.enter_context(tc.tile_pool(name="grouped_pool", bufs=3))
        attn_pool = ctx.enter_context(tc.tile_pool(name="attn_pool", bufs=2))
        out_pool = ctx.enter_context(tc.tile_pool(name="out_pool", bufs=OUT_BUFFERS))
        psum_v = ctx.enter_context(tc.psum_pool(name="psum_v", bufs=4))
        psum_o = ctx.enter_context(tc.psum_pool(name="psum_o", bufs=4))
        ctx.enter_context(tc.manual_schedule())

        w_raw = resident.tile([P, PACK, CHANNELS], BF16)
        attn_raw = [
            resident.tile([P, PACK * CHANNELS], BF16, name="attn_raw%d" % b) for b in range(SAMPLES)
        ]

        def load_attn(b):
            nc.sync.dma_start(
                out=attn_raw[b][:], in_=attn[b, 0].rearrange("(p g) j -> p (g j)", g=PACK)
            )

        x_part = []

        def load_x(b, first, voxels):
            piece = resident.tile([P, PACK, voxels], BF16, name="x_piece%d_%d" % (b, first))
            nc.sync.dma_start(out=piece[:], in_=x_rows[b, :, :, first : first + voxels])
            return piece

        nc.sync.dma_start(out=w_raw[:], in_=w_rows)
        x_part.append([(h * HALF, HALF, load_x(0, h * HALF, HALF)[:]) for h in range(2)])
        x_part.append([(0, CHUNK, load_x(0, CHUNK, CHUNK)[:])])
        load_attn(0)
        for q in range(2, CHUNKS_PER_SAMPLE):
            x_part.append([(0, CHUNK, load_x(0, q * CHUNK, CHUNK)[:])])
        for b in range(1, SAMPLES):
            pieces = 2 if b == 1 else 1
            span = VOXELS // pieces
            for h in range(pieces):
                piece = load_x(b, h * span, span)
                for q in range(span // CHUNK):
                    x_part.append([(0, CHUNK, piece[:, :, q * CHUNK : (q + 1) * CHUNK])])
            load_attn(b)

        identity = resident.tile([P, P], F32)
        make_identity(nc, identity[:])

        zeros = resident.tile([P, CHUNK], BF16)
        nc.gpsimd.memset(zeros[:], 0.0)
        warm_bank = psum_v.tile([P, CHUNK], F32, name="v_bank")
        for i in range(WARM_MATMULS):
            nc.tensor.matmul(warm_bank[:], lhsT=zeros[:, :P], rhs=zeros[:], start=True, stop=True)

        w_grouped = resident.tile([P, PACK, P, PACK], BF16, align_bytes=64)
        w_codes = resident.tile([P, CHANNELS], U32, align_bytes=64)
        w_scales = resident.tile([P, CHANNELS], U8, align_bytes=64)

        def regroup_w():
            dst = w_grouped[:].rearrange("p s m t -> p m t s")
            src = w_raw[:].rearrange("p t (m s) -> p m t s", s=PACK)
            nc.scalar.copy(out=dst[:, : P // 2], in_=src[:, : P // 2])
            nc.vector.tensor_copy(out=dst[:, P // 2 :], in_=src[:, P // 2 :])

        def quantise_w():
            nc.vector.quantize_mx(
                out=w_codes[:].bitcast(FP8X4),
                scales=w_scales[:],
                in_=w_grouped[:].rearrange("p s m t -> p (s m t)"),
            )

        attn_grouped = {}
        attn_mx = {}

        def transpose_attn(b):
            words = attn_raw[b][:].bitcast(F32).rearrange("p (g m u) -> p g u m", g=PACK, u=2)
            grouped = attn_pool.tile([P, PACK * P * PACK], BF16, align_bytes=64, name="attn_grouped")
            grouped_words = grouped[:].bitcast(F32).rearrange("m (g p u) -> m g p u", g=PACK, u=2)
            for half in range(2):
                bank = psum_o.tile([P, 2, 2, P], F32, tag="bank", name="attn_bank")
                for g in range(2):
                    for u in range(2):
                        nc.tensor.transpose(bank[:, g, u, :], words[:, 2 * half + g, u, :], identity[:])
                nc.scalar.copy(
                    out=grouped_words[:, 2 * half : 2 * half + 2, :, :],
                    in_=bank[:].rearrange("m g u p -> m g p u"),
                )
            attn_grouped[b] = grouped

        def quantise_attn(b):
            codes = attn_pool.tile([P, CHANNELS], U32, align_bytes=64, name="attn_codes")
            scales = attn_pool.tile([P, CHANNELS], U8, align_bytes=64, name="attn_scales")
            nc.vector.quantize_mx(out=codes[:].bitcast(FP8X4), scales=scales[:], in_=attn_grouped[b][:])
            attn_mx[b] = (codes, scales)

        x_grouped = {}
        x_mx = {}
        v_banks = {}
        v_mx = {}
        out_banks = {}

        def vector_banks(k):
            if k < 2:
                return k
            if k % CHUNKS_PER_SAMPLE == 3 or k == 13:
                return 3
            return 2

        def gpsimd_voxels(k):
            return GPSIMD_VOXELS * vector_banks(k - 2) // 2

        def regroup_x(k, pieces=None):
            if k not in x_grouped:
                x_grouped[k] = grouped_pool.tile([P, CHUNK, PACK], BF16, align_bytes=64, name="grouped")
            grouped = x_grouped[k]
            for first, voxels, view in x_part[k] if pieces is None else [x_part[k][i] for i in pieces]:
                split = voxels
                if k >= GPSIMD_FIRST_CHUNK:
                    split = voxels - gpsimd_voxels(k)
                    nc.gpsimd.tensor_scalar(
                        out=grouped[:, first + split : first + voxels, :],
                        in0=view[:, :, split:].rearrange("p t n -> p n t"),
                        scalar1=1.0,
                        scalar2=0.0,
                        op0=mybir.AluOpType.mult,
                        op1=mybir.AluOpType.add,
                    )
                copy = nc.scalar.copy if (k == 0 and first > 0) else nc.vector.tensor_copy
                copy(
                    out=grouped[:, first : first + split, :].rearrange("p (c i) t -> p c t i", i=4),
                    in_=view[:, :, :split].rearrange("p t (c i) -> p c t i", i=4),
                )

        def quantise_x(k, pieces=None):
            if k not in x_mx:
                x_codes = stream.tile([P, CHUNK], U32, align_bytes=64, name="x_codes")
                x_scales = stream.tile([P, CHUNK], U8, align_bytes=64, name="x_scales")
                x_mx[k] = (x_codes, x_scales)
            codes, scales = x_mx[k]
            for first, voxels, view in x_part[k] if pieces is None else [x_part[k][i] for i in pieces]:
                nc.vector.quantize_mx(
                    out=codes[:, first : first + voxels].bitcast(FP8X4),
                    scales=scales[:, first : first + voxels],
                    in_=x_grouped[k][:, first : first + voxels, :].rearrange("p n t -> p (n t)"),
                )

        def first_product(k):
            codes, scales = x_mx[k]
            v_banks[k] = []
            for r in range(PACK):
                voxels = slice(r * SLICE, (r + 1) * SLICE)
                bank = psum_v.tile([P, PACK, SLICE], F32, name="v_bank")
                for s in range(PACK):
                    tile_s = slice(s * P, (s + 1) * P)
                    nc.tensor.matmul_mx(
                        out=bank[:, s, :],
                        lhsT=w_codes[:, tile_s].bitcast(FP8X4),
                        lhsT_scale=w_scales[:, tile_s],
                        rhs=codes[:, voxels].bitcast(FP8X4),
                        rhs_scale=scales[:, voxels],
                        start=True,
                        stop=True,
                    )
                v_banks[k].append(bank)

        v_grouped = {}

        def round_v(k):
            grouped = grouped_pool.tile([P, CHUNK, PACK], BF16, align_bytes=64, name="grouped")
            scalar_banks = PACK - vector_banks(k)
            for r in range(PACK):
                dst = grouped[:, r * SLICE : (r + 1) * SLICE, :]
                src = v_banks[k][r][:].rearrange("m s n -> m n s")
                if r < scalar_banks:
                    nc.scalar.copy(out=dst, in_=src)
                else:
                    nc.vector.tensor_copy(out=dst, in_=src)
            v_grouped[k] = grouped

        def quantise_v(k):
            codes = stream.tile([P, CHUNK], U32, align_bytes=64, name="v_codes")
            scales = stream.tile([P, CHUNK], U8, align_bytes=64, name="v_scales")
            nc.vector.quantize_mx(
                out=codes[:].bitcast(FP8X4),
                scales=scales[:],
                in_=v_grouped[k][:].rearrange("m n s -> m (n s)"),
            )
            v_mx[k] = (codes, scales)

        def second_product(k):
            a_codes, a_scales = attn_mx[k // CHUNKS_PER_SAMPLE]
            codes, scales = v_mx[k]
            out_banks[k] = []
            for g in range(PACK):
                tile_g = slice(g * P, (g + 1) * P)
                bank = psum_o.tile([P, CHUNK], F32, tag="bank", name="out_bank")
                nc.tensor.matmul_mx(
                    out=bank[:],
                    lhsT=a_codes[:, tile_g].bitcast(FP8X4),
                    lhsT_scale=a_scales[:, tile_g],
                    rhs=codes[:].bitcast(FP8X4),
                    rhs_scale=scales[:],
                    start=True,
                    stop=True,
                )
                out_banks[k].append(bank)

        def store_out(k):
            b, q = divmod(k, CHUNKS_PER_SAMPLE)
            for g in range(PACK):
                result = out_pool.tile([P, CHUNK], F32, name="result")
                if k == STEPS - 1 and g % 2 == 1:
                    nc.vector.tensor_copy(out=result[:], in_=out_banks[k][g][:])
                else:
                    nc.scalar.copy(out=result[:], in_=out_banks[k][g][:])
                nc.sync.dma_start(out=out_rows[b, :, g, q * CHUNK : (q + 1) * CHUNK], in_=result[:])

        regroup_w()
        regroup_x(0, [0])
        quantise_w()
        quantise_x(0, [0])
        regroup_x(0, [1])
        quantise_x(0, [1])
        first_product(0)
        regroup_x(1)
        quantise_x(1)
        for k in range(STEPS):
            b, q = divmod(k, CHUNKS_PER_SAMPLE)
            round_v(k)
            if k == 0:
                transpose_attn(0)
            if k + 1 < STEPS:
                first_product(k + 1)
            if k >= 1:
                store_out(k - 1)
            if q == 2 and b + 1 < SAMPLES:
                transpose_attn(b + 1)
            if k == 0:
                quantise_v(k)
            if k + 2 < STEPS:
                regroup_x(k + 2)
            if k == 0:
                quantise_attn(0)
            if q == 3 and b + 1 < SAMPLES:
                quantise_attn(b + 1)
            if k > 0:
                quantise_v(k)
            second_product(k)
            if k + 2 < STEPS:
                quantise_x(k + 2)
        store_out(STEPS - 1)
